import numpy as np
import ml_dtypes

BF16 = ml_dtypes.bfloat16


def bf(x):
    return np.asarray(x, np.float32).astype(BF16)


def f32(x):
    return np.asarray(x, np.float32)


def f64(x):
    return np.asarray(x).astype(np.float64)


def striped(idx):
    return np.tile(idx.reshape(-1, 16).T, (8, 1))


B, K, Q, S, N = 128, 3, 7, 2048, 2048
EPS = 1e-8


def setup_inputs():
    return {"verts": f32(np.random.standard_normal((K * B, S))), "cams": f32(np.random.standard_normal((B, Q))), "offs": striped(np.random.permutation(np.tile(np.arange(S), 2))[:N])}


def reference(verts, cams, offs):
    idx = offs[:16].T.reshape(-1)
    p = f64(verts).reshape(K, B, S)[:, :, idx]
    cm = f64(cams)
    sc, tx, ty = cm[:, 0:1], cm[:, 1:2], cm[:, 2:3]
    quat = cm[:, 3:]
    quat = quat / (np.sqrt(np.sum(quat * quat, axis=1, keepdims=True)) + EPS)
    qw, qx, qy, qz = quat[:, 0:1], quat[:, 1:2], quat[:, 2:3], quat[:, 3:4]
    r00 = 1.0 - 2.0 * (qy * qy + qz * qz)
    r01 = 2.0 * (qx * qy - qw * qz)
    r02 = 2.0 * (qx * qz + qw * qy)
    r10 = 2.0 * (qx * qy + qw * qz)
    r11 = 1.0 - 2.0 * (qx * qx + qz * qz)
    r12 = 2.0 * (qy * qz - qw * qx)
    u = sc * (r00 * p[0] + r01 * p[1] + r02 * p[2]) + tx
    v = sc * (r10 * p[0] + r11 * p[1] + r12 * p[2]) + ty
    return np.concatenate([u, v], axis=0)

@@ -1,0 +1,172 @@
+import concourse.mybir as mybir
+from concourse.masks import make_identity
+
+F32 = mybir.dt.float32
+U16 = mybir.dt.uint16
+ALU = mybir.AluOpType
+ACT = mybir.ActivationFunctionType
+
+SAMPLES = 128
+VERTICES = 2048
+PICKS = 2048
+PIECES = (512, 512, 512, 384, 128)
+WIDEST = max(PIECES)
+assert sum(PIECES) == PICKS and all(width % 32 == 0 for width in PIECES)
+EPS = 1e-8
+TINY = 1e-30
+QW, QX, QY, QZ = 0, 1, 2, 3
+
+
+def tile_corrlosschamfer_kernel(tc, verts, cams, offs, out):
+    nc = tc.nc
+    with (
+        tc.tile_pool(name="held", bufs=1) as held,
+        tc.tile_pool(name="work", bufs=len(PIECES)) as work,
+        tc.psum_pool(name="sums", bufs=len(PIECES)) as sums,
+    ):
+        cam = held.tile([SAMPLES, 7], F32, name="cam")
+        nc.sync.dma_start(cam[:], cams)
+        coords = [held.tile([SAMPLES, VERTICES], F32, name=f"coord{k}") for k in range(3)]
+        nc.sync.dma_start(coords[0][:], verts[0:SAMPLES, :])
+        offsets = held.tile([128, PICKS // 16], U16, name="offsets")
+        nc.sync.dma_start(offsets[:], offs)
+        for k in (1, 2):
+            nc.sync.dma_start(coords[k][:], verts[k * SAMPLES : (k + 1) * SAMPLES, :])
+        scale = cam[:, 0:1]
+        shift = [cam[:, 1:2], cam[:, 2:3]]
+        quat = cam[:, 3:7]
+
+        identity = held.tile([SAMPLES, SAMPLES], F32, name="identity")
+        make_identity(nc, identity[:])
+        half = held.tile([SAMPLES, 1], F32, name="half")
+        nc.gpsimd.memset(half[:], 0.5)
+        diagonal = held.tile([SAMPLES, 6], F32, name="diagonal")
+        nc.gpsimd.memset(diagonal[:], 0.0)
+        nc.gpsimd.memset(diagonal[:, 0:1], 1.0)
+        nc.gpsimd.memset(diagonal[:, 3:4], 1.0)
+        diagonal_eps = held.tile([SAMPLES, 6], F32, name="diagonal_eps")
+        nc.gpsimd.memset(diagonal_eps[:], 0.0)
+        nc.gpsimd.memset(diagonal_eps[:, 0:1], EPS)
+        nc.gpsimd.memset(diagonal_eps[:, 3:4], EPS)
+        rootless_tile = held.tile([SAMPLES, 9], F32, name="rootless_tile")
+        nc.gpsimd.memset(rootless_tile[:], TINY)
+        rootless_and_floor = rootless_tile[:].rearrange("p (k c) -> p k c", c=3)
+        rootless = rootless_and_floor[:, :, 0:2]
+        ones = held.tile([SAMPLES, WIDEST], F32, name="ones")
+        nc.gpsimd.memset(ones[:], 1.0)
+
+        def by_k(six):
+            return six[:].rearrange("p (k r) -> p k r", r=2)
+
+        pair = held.tile([SAMPLES, 16], F32, name="pair")
+        nc.vector.tensor_tensor(
+            pair[:].rearrange("p (i j) -> p i j", i=4),
+            quat.unsqueeze(2).to_broadcast([SAMPLES, 4, 4]),
+            quat.unsqueeze(1).to_broadcast([SAMPLES, 4, 4]),
+            ALU.mult,
+        )
+        sumsq = held.tile([SAMPLES, 1], F32, name="sumsq")
+        nc.vector.reduce_sum(sumsq[:], pair[:, 0:16:5], axis=mybir.AxisListType.X)
+        norm = held.tile([SAMPLES, 1], F32, name="norm")
+        nc.gpsimd.tensor_tensor(norm[:], sumsq[:], half[:], ALU.pow)
+
+        base = held.tile([SAMPLES, 1], F32, name="base")
+        nc.vector.tensor_scalar(base[:], sumsq[:], 0.5, 0.5 * EPS * EPS, ALU.mult, ALU.add)
+
+        def pr(i, j):
+            return pair[:, 4 * i + j : 4 * i + j + 1]
+
+        mixes = held.tile([SAMPLES, 6], F32, name="mixes")
+        mix = {(r, k): mixes[:, 2 * k + r : 2 * k + r + 1] for r in range(2) for k in range(3)}
+        nc.vector.tensor_scalar(mix[0, 0], pr(QY, QY), pr(QZ, QZ), -1.0, ALU.add, ALU.mult)
+        nc.vector.tensor_tensor(mix[0, 1], pr(QX, QY), pr(QW, QZ), ALU.subtract)
+        nc.vector.tensor_tensor(mix[0, 2], pr(QX, QZ), pr(QW, QY), ALU.add)
+        nc.vector.tensor_tensor(mix[1, 0], pr(QX, QY), pr(QW, QZ), ALU.add)
+        nc.vector.tensor_scalar(mix[1, 1], pr(QX, QX), pr(QZ, QZ), -1.0, ALU.add, ALU.mult)
+        nc.vector.tensor_tensor(mix[1, 2], pr(QY, QZ), pr(QW, QX), ALU.subtract)
+
+        nc.vector.scalar_tensor_tensor(
+            rootless, by_k(diagonal), base[:, 0:1], by_k(mixes), ALU.mult, ALU.add
+        )
+        larger = held.tile([SAMPLES, 3], F32, name="larger")
+        nc.vector.tensor_reduce(
+            larger[:], rootless_and_floor, axis=mybir.AxisListType.X, op=ALU.max, apply_absolute_value=True
+        )
+        inv_base = held.tile([SAMPLES, 1], F32, name="inv_base")
+        nc.vector.reciprocal(inv_base[:], base[:])
+
+        spread = [held.tile([SAMPLES, WIDEST], F32, name=f"spread{k}") for k in range(3)]
+        nc.vector.tensor_scalar(
+            spread[0][:], ones[:], larger[:, 0:1], inv_base[:, 0:1], ALU.mult, ALU.mult
+        )
+        for k in (1, 2):
+            nc.scalar.activation(
+                spread[k][:],
+                larger[:, k : k + 1].to_broadcast([SAMPLES, WIDEST]),
+                ACT.Identity,
+                scale=inv_base[:, 0:1],
+            )
+
+        inv_larger = held.tile([SAMPLES, 3], F32, name="inv_larger")
+        nc.vector.reciprocal(inv_larger[:], larger[:])
+        scale_by_pivot = held.tile([SAMPLES, 3], F32, name="scale_by_pivot")
+        nc.vector.tensor_scalar(
+            scale_by_pivot[:], inv_larger[:], scale, base[:, 0:1], ALU.mult, ALU.mult
+        )
+        numer = held.tile([SAMPLES, 6], F32, name="numer")
+        nc.vector.scalar_tensor_tensor(
+            by_k(numer), by_k(diagonal_eps), norm[:, 0:1], rootless, ALU.mult, ALU.add
+        )
+        halved = held.tile([SAMPLES, 1], F32, name="halved")
+        nc.vector.scalar_tensor_tensor(halved[:], norm[:], EPS, base[:], ALU.mult, ALU.add)
+        inv_halved = held.tile([SAMPLES, 1], F32, name="inv_halved")
+        nc.vector.reciprocal(inv_halved[:], halved[:])
+        factors = held.tile([SAMPLES, 6], F32, name="factors")
+        nc.vector.scalar_tensor_tensor(
+            by_k(factors),
+            by_k(numer),
+            inv_halved[:, 0:1],
+            scale_by_pivot[:].unsqueeze(2).to_broadcast([SAMPLES, 3, 2]),
+            ALU.mult,
+            ALU.mult,
+        )
+        factor = {(r, k): factors[:, 2 * k + r : 2 * k + r + 1] for r in range(2) for k in range(3)}
+
+        weights0 = []
+        for k in range(3):
+            weights0.append(held.tile([SAMPLES, SAMPLES], F32, name=f"weights0{k}"))
+            nc.scalar.activation(weights0[k][:], identity[:], ACT.Identity, scale=factor[0, k])
+
+        first = 0
+        for width in PIECES:
+            columns = slice(first, first + width)
+            piece_offsets = offsets[:, first // 16 : (first + width) // 16]
+            total0 = sums.tile([SAMPLES, width], F32, name="total0")
+            picked = []
+            for k in range(3):
+                picked.append(work.tile([SAMPLES, width], F32, name=f"picked{k}"))
+                nc.vector.tensor_tensor(
+                    picked[k][:], coords[k][:].indirect(piece_offsets), spread[k][:, 0:width], ALU.mult
+                )
+                nc.tensor.matmul(
+                    total0[:], weights0[k][:], picked[k][:], start=(k == 0), stop=(k == 2)
+                )
+            image = work.tile([SAMPLES, 2, width], F32, name="image")
+            one_term = work.tile([SAMPLES, width], F32, name="one_term")
+            nc.scalar.activation(
+                one_term[:], picked[0][:], ACT.Identity, bias=shift[1], scale=factor[1, 0]
+            )
+            two_terms = work.tile([SAMPLES, width], F32, name="two_terms")
+            nc.vector.scalar_tensor_tensor(
+                two_terms[:], picked[1][:], factor[1, 1], one_term[:], ALU.mult, ALU.add
+            )
+            nc.vector.scalar_tensor_tensor(
+                image[:, 1, :], picked[2][:], factor[1, 2], two_terms[:], ALU.mult, ALU.add
+            )
+            nc.scalar.activation(image[:, 0, :], total0[:], ACT.Identity, bias=shift[0])
+            if first + width < PICKS:
+                for r in (1, 0):
+                    nc.sync.dma_start(out[r * SAMPLES : (r + 1) * SAMPLES, columns], image[:, r, :])
+            else:
+                nc.sync.dma_start(out.rearrange("(r p) c -> p r c", r=2)[:, :, columns], image[:])
+            first += width

@@ -7,6 +7,7 @@ ALU = mybir.AluOpType
 ACT = mybir.ActivationFunctionType
 
 SAMPLES = 128
+GROUP = 32
 VERTICES = 2048
 PICKS = 2048
 PIECES = (512, 512, 512, 384, 128)
@@ -15,6 +16,15 @@ assert sum(PIECES) == PICKS and all(width % 32 == 0 for width in PIECES)
 EPS = 1e-8
 TINY = 1e-30
 QW, QX, QY, QZ = 0, 1, 2, 3
+WINDOWS = (
+    ((0, 0), (0, 1), (1, 0), (2, 0)),
+    ((1, 1), (1, 2), (2, 1), (0, 2)),
+    ((2, 2), (2, 3), (0, 3), (1, 3)),
+)
+
+
+def windows_of(group):
+    return [t for t in range(3) if any(g == group for k, g in WINDOWS[t])]
 
 
 def tile_corrlosschamfer_kernel(tc, verts, cams, offs, out):
@@ -22,38 +32,56 @@ def tile_corrlosschamfer_kernel(tc, verts, cams, offs, out):
     with (
         tc.tile_pool(name="held", bufs=1) as held,
         tc.tile_pool(name="work", bufs=len(PIECES)) as work,
-        tc.psum_pool(name="sums", bufs=len(PIECES)) as sums,
+        tc.psum_pool(name="spread_out", bufs=1) as spread_out,
+        tc.psum_pool(name="sums", bufs=3) as sums,
     ):
         cam = held.tile([SAMPLES, 7], F32, name="cam")
         nc.sync.dma_start(cam[:], cams)
-        coords = [held.tile([SAMPLES, VERTICES], F32, name=f"coord{k}") for k in range(3)]
-        nc.sync.dma_start(coords[0][:], verts[0:SAMPLES, :])
+        windows = [held.tile([128, VERTICES], F32, name=f"window{t}") for t in range(3)]
         offsets = held.tile([128, PICKS // 16], U16, name="offsets")
+
+        def load_window(t):
+            for first, count in ((0, 2), (2, 1), (3, 1)):
+                k, group = WINDOWS[t][first]
+                row = k * SAMPLES + group * GROUP
+                nc.sync.dma_start(
+                    windows[t][first * GROUP : (first + count) * GROUP, :],
+                    verts[row : row + count * GROUP, :],
+                )
+
+        load_window(0)
         nc.sync.dma_start(offsets[:], offs)
-        for k in (1, 2):
-            nc.sync.dma_start(coords[k][:], verts[k * SAMPLES : (k + 1) * SAMPLES, :])
+        load_window(1)
+        load_window(2)
+        shift = held.tile([128, 2], F32, name="shift")
+        for r in range(2):
+            nc.sync.dma_start(
+                shift[64 * r : 64 * (r + 1), :],
+                cams.rearrange("(h p) c -> p h c", h=2)[:, :, 1 + r],
+            )
         scale = cam[:, 0:1]
-        shift = [cam[:, 1:2], cam[:, 2:3]]
         quat = cam[:, 3:7]
 
         identity = held.tile([SAMPLES, SAMPLES], F32, name="identity")
         make_identity(nc, identity[:])
         half = held.tile([SAMPLES, 1], F32, name="half")
         nc.gpsimd.memset(half[:], 0.5)
-        diagonal = held.tile([SAMPLES, 6], F32, name="diagonal")
-        nc.gpsimd.memset(diagonal[:], 0.0)
-        nc.gpsimd.memset(diagonal[:, 0:1], 1.0)
-        nc.gpsimd.memset(diagonal[:, 3:4], 1.0)
         diagonal_eps = held.tile([SAMPLES, 6], F32, name="diagonal_eps")
         nc.gpsimd.memset(diagonal_eps[:], 0.0)
-        nc.gpsimd.memset(diagonal_eps[:, 0:1], EPS)
-        nc.gpsimd.memset(diagonal_eps[:, 3:4], EPS)
+        nc.gpsimd.memset(diagonal_eps[:, 0:4:3], EPS)
         rootless_tile = held.tile([SAMPLES, 9], F32, name="rootless_tile")
         nc.gpsimd.memset(rootless_tile[:], TINY)
         rootless_and_floor = rootless_tile[:].rearrange("p (k c) -> p k c", c=3)
         rootless = rootless_and_floor[:, :, 0:2]
-        ones = held.tile([SAMPLES, WIDEST], F32, name="ones")
+        ones = held.tile([128, WIDEST], F32, name="ones")
         nc.gpsimd.memset(ones[:], 1.0)
+        pattern = []
+        for t in range(3):
+            pattern.append(held.tile([128, 2, GROUP], F32, name=f"pattern{t}"))
+            nc.vector.memset(pattern[t][:], 0.0)
+            for j in range(4):
+                block = slice(j * GROUP, (j + 1) * GROUP)
+                nc.vector.tensor_copy(pattern[t][block, WINDOWS[t][j][1] % 2, :], identity[block, block])
 
         def by_k(six):
             return six[:].rearrange("p (k r) -> p k r", r=2)
@@ -70,23 +98,32 @@ def tile_corrlosschamfer_kernel(tc, verts, cams, offs, out):
         norm = held.tile([SAMPLES, 1], F32, name="norm")
         nc.gpsimd.tensor_tensor(norm[:], sumsq[:], half[:], ALU.pow)
 
+        def pr(i, j):
+            return 4 * i + j
+
+        def mixed(r, k):
+            return 3 * k + r
+
+        nc.vector.tensor_tensor(
+            rootless_tile[:, mixed(1, 0) : mixed(0, 2) + 1 : 5],
+            pair[:, pr(QX, QY) : pr(QX, QZ) + 1],
+            pair[:, pr(QY, QW) : pr(QZ, QW) + 1 : 4][:, ::-1],
+            ALU.add,
+        )
+        nc.vector.tensor_tensor(
+            rootless_tile[:, mixed(0, 1) : mixed(1, 2) + 1 : 4],
+            pair[:, pr(QX, QY) : pr(QY, QZ) + 1 : 5],
+            pair[:, pr(QW, QX) : pr(QW, QZ) + 1 : 2][:, ::-1],
+            ALU.subtract,
+        )
         base = held.tile([SAMPLES, 1], F32, name="base")
         nc.vector.tensor_scalar(base[:], sumsq[:], 0.5, 0.5 * EPS * EPS, ALU.mult, ALU.add)
-
-        def pr(i, j):
-            return pair[:, 4 * i + j : 4 * i + j + 1]
-
-        mixes = held.tile([SAMPLES, 6], F32, name="mixes")
-        mix = {(r, k): mixes[:, 2 * k + r : 2 * k + r + 1] for r in range(2) for k in range(3)}
-        nc.vector.tensor_scalar(mix[0, 0], pr(QY, QY), pr(QZ, QZ), -1.0, ALU.add, ALU.mult)
-        nc.vector.tensor_tensor(mix[0, 1], pr(QX, QY), pr(QW, QZ), ALU.subtract)
-        nc.vector.tensor_tensor(mix[0, 2], pr(QX, QZ), pr(QW, QY), ALU.add)
-        nc.vector.tensor_tensor(mix[1, 0], pr(QX, QY), pr(QW, QZ), ALU.add)
-        nc.vector.tensor_scalar(mix[1, 1], pr(QX, QX), pr(QZ, QZ), -1.0, ALU.add, ALU.mult)
-        nc.vector.tensor_tensor(mix[1, 2], pr(QY, QZ), pr(QW, QX), ALU.subtract)
-
-        nc.vector.scalar_tensor_tensor(
-            rootless, by_k(diagonal), base[:, 0:1], by_k(mixes), ALU.mult, ALU.add
+        squares = held.tile([SAMPLES, 2], F32, name="squares")
+        nc.vector.tensor_scalar(
+            squares[:], pair[:, pr(QX, QX) : pr(QY, QY) + 1 : 5], pair[:, pr(QZ, QZ) : pr(QZ, QZ) + 1], None, ALU.add
+        )
+        nc.vector.tensor_scalar(
+            rootless_tile[:, mixed(0, 0) : mixed(1, 1) + 1 : 4], squares[:, ::-1], -1.0, base[:, 0:1], ALU.mult, ALU.add
         )
         larger = held.tile([SAMPLES, 3], F32, name="larger")
         nc.vector.tensor_reduce(
@@ -94,29 +131,34 @@ def tile_corrlosschamfer_kernel(tc, verts, cams, offs, out):
         )
         inv_base = held.tile([SAMPLES, 1], F32, name="inv_base")
         nc.vector.reciprocal(inv_base[:], base[:])
+        pivots = held.tile([SAMPLES, 3], F32, name="pivots")
+        nc.vector.tensor_scalar(pivots[:], larger[:], inv_base[:, 0:1], None, ALU.mult)
 
-        spread = [held.tile([SAMPLES, WIDEST], F32, name=f"spread{k}") for k in range(3)]
-        nc.vector.tensor_scalar(
-            spread[0][:], ones[:], larger[:, 0:1], inv_base[:, 0:1], ALU.mult, ALU.mult
-        )
-        for k in (1, 2):
-            nc.scalar.activation(
-                spread[k][:],
-                larger[:, k : k + 1].to_broadcast([SAMPLES, WIDEST]),
-                ACT.Identity,
-                scale=inv_base[:, 0:1],
-            )
+        def to_windows(dest, source, columns):
+            for t in range(3):
+                for j in range(4):
+                    k, group = WINDOWS[t][j]
+                    nc.tensor.matmul(
+                        dest[j * GROUP : (j + 1) * GROUP, t, :],
+                        identity[:, group * GROUP : (group + 1) * GROUP],
+                        source[:, columns * k : columns * (k + 1)],
+                        start=True,
+                        stop=True,
+                    )
+
+        pivot = spread_out.tile([128, 3, 1], F32, name="pivot")
+        to_windows(pivot, pivots, 1)
+        spread = [held.tile([128, WIDEST], F32, name=f"spread{t}") for t in range(3)]
+        nc.vector.tensor_scalar(spread[0][:], ones[:], pivot[:, 0, :], None, ALU.mult)
+        for t in (1, 2):
+            nc.scalar.activation(spread[t][:], pivot[:, t, :].to_broadcast([128, WIDEST]), ACT.Identity)
 
         inv_larger = held.tile([SAMPLES, 3], F32, name="inv_larger")
         nc.vector.reciprocal(inv_larger[:], larger[:])
         scale_by_pivot = held.tile([SAMPLES, 3], F32, name="scale_by_pivot")
-        nc.vector.tensor_scalar(
-            scale_by_pivot[:], inv_larger[:], scale, base[:, 0:1], ALU.mult, ALU.mult
-        )
+        nc.vector.tensor_scalar(scale_by_pivot[:], inv_larger[:], scale, base[:, 0:1], ALU.mult, ALU.mult)
         numer = held.tile([SAMPLES, 6], F32, name="numer")
-        nc.vector.scalar_tensor_tensor(
-            by_k(numer), by_k(diagonal_eps), norm[:, 0:1], rootless, ALU.mult, ALU.add
-        )
+        nc.vector.scalar_tensor_tensor(by_k(numer), by_k(diagonal_eps), norm[:, 0:1], rootless, ALU.mult, ALU.add)
         halved = held.tile([SAMPLES, 1], F32, name="halved")
         nc.vector.scalar_tensor_tensor(halved[:], norm[:], EPS, base[:], ALU.mult, ALU.add)
         inv_halved = held.tile([SAMPLES, 1], F32, name="inv_halved")
@@ -130,43 +172,40 @@ def tile_corrlosschamfer_kernel(tc, verts, cams, offs, out):
             ALU.mult,
             ALU.mult,
         )
-        factor = {(r, k): factors[:, 2 * k + r : 2 * k + r + 1] for r in range(2) for k in range(3)}
+        factor_psum = spread_out.tile([128, 3, 2], F32, name="factor_psum")
+        to_windows(factor_psum, factors, 2)
+        factor = held.tile([128, 3, 2], F32, name="factor")
+        nc.scalar.activation(factor[:], factor_psum[:], ACT.Identity)
+        weights = []
+        for t in range(3):
+            weights.append(held.tile([128, 2, 2, GROUP], F32, name=f"weights{t}"))
+            for r in range(2):
+                nc.scalar.activation(weights[t][:, r, :, :], pattern[t][:], ACT.Identity, scale=factor[:, t, r : r + 1])
 
-        weights0 = []
-        for k in range(3):
-            weights0.append(held.tile([SAMPLES, SAMPLES], F32, name=f"weights0{k}"))
-            nc.scalar.activation(weights0[k][:], identity[:], ACT.Identity, scale=factor[0, k])
-
+        out_u_v = out.rearrange("(r h p) c -> r p h c", r=2, h=2)
         first = 0
         for width in PIECES:
             columns = slice(first, first + width)
             piece_offsets = offsets[:, first // 16 : (first + width) // 16]
-            total0 = sums.tile([SAMPLES, width], F32, name="total0")
-            picked = []
-            for k in range(3):
-                picked.append(work.tile([SAMPLES, width], F32, name=f"picked{k}"))
+            total = [sums.tile([128, width], F32, name=f"total{h}") for h in range(2)]
+            for t in range(3):
+                picked = work.tile([128, width], F32, name=f"picked{t}")
                 nc.vector.tensor_tensor(
-                    picked[k][:], coords[k][:].indirect(piece_offsets), spread[k][:, 0:width], ALU.mult
+                    picked[:], windows[t][:].indirect(piece_offsets), spread[t][:, 0:width], ALU.mult
                 )
-                nc.tensor.matmul(
-                    total0[:], weights0[k][:], picked[k][:], start=(k == 0), stop=(k == 2)
-                )
-            image = work.tile([SAMPLES, 2, width], F32, name="image")
-            one_term = work.tile([SAMPLES, width], F32, name="one_term")
-            nc.scalar.activation(
-                one_term[:], picked[0][:], ACT.Identity, bias=shift[1], scale=factor[1, 0]
-            )
-            two_terms = work.tile([SAMPLES, width], F32, name="two_terms")
-            nc.vector.scalar_tensor_tensor(
-                two_terms[:], picked[1][:], factor[1, 1], one_term[:], ALU.mult, ALU.add
-            )
-            nc.vector.scalar_tensor_tensor(
-                image[:, 1, :], picked[2][:], factor[1, 2], two_terms[:], ALU.mult, ALU.add
-            )
-            nc.scalar.activation(image[:, 0, :], total0[:], ACT.Identity, bias=shift[0])
-            if first + width < PICKS:
-                for r in (1, 0):
-                    nc.sync.dma_start(out[r * SAMPLES : (r + 1) * SAMPLES, columns], image[:, r, :])
-            else:
-                nc.sync.dma_start(out.rearrange("(r p) c -> p r c", r=2)[:, :, columns], image[:])
+                for group in sorted({g for k, g in WINDOWS[t]}):
+                    for r in range(2):
+                        quadrant = 2 * r + group % 2
+                        nc.tensor.matmul(
+                            total[group // 2][quadrant * GROUP : (quadrant + 1) * GROUP, :],
+                            weights[t][:, r, group % 2, :],
+                            picked[:],
+                            start=(t == windows_of(group)[0]),
+                            stop=(t == windows_of(group)[-1]),
+                        )
+            image = work.tile([128, 2, width], F32, name="image")
+            for h in range(2):
+                nc.scalar.activation(image[:, h, :], total[h][:], ACT.Identity, bias=shift[:, h : h + 1])
+            for r in range(2):
+                nc.sync.dma_start(out_u_v[r][:, :, columns], image[64 * r : 64 * (r + 1), :, :])
             first += width

@@ -5,26 +5,26 @@ F32 = mybir.dt.float32
 U16 = mybir.dt.uint16
 ALU = mybir.AluOpType
 ACT = mybir.ActivationFunctionType
+X = mybir.AxisListType.X
 
 SAMPLES = 128
 GROUP = 32
+BLOCKS = 4
 VERTICES = 2048
 PICKS = 2048
-PIECES = (512, 512, 512, 384, 128)
+PIECES = (128, 384, 512, 512, 384, 128)
 WIDEST = max(PIECES)
 assert sum(PIECES) == PICKS and all(width % 32 == 0 for width in PIECES)
 EPS = 1e-8
 TINY = 1e-30
 QW, QX, QY, QZ = 0, 1, 2, 3
 WINDOWS = (
-    ((0, 0), (0, 1), (1, 0), (2, 0)),
-    ((1, 1), (1, 2), (2, 1), (0, 2)),
-    ((2, 2), (2, 3), (0, 3), (1, 3)),
+    ((0, 0), (1, 0), (2, 0), (0, 1)),
+    ((0, 2), (1, 1), (2, 1), (1, 2)),
+    ((0, 3), (1, 3), (2, 3), (2, 2)),
 )
-
-
-def windows_of(group):
-    return [t for t in range(3) if any(g == group for k, g in WINDOWS[t])]
+FIRST_WINDOW = {0: 0, 1: 0, 2: 1, 3: 2}
+LAST_WINDOW = {0: 0, 1: 1, 2: 2, 3: 2}
 
 
 def tile_corrlosschamfer_kernel(tc, verts, cams, offs, out):
@@ -32,160 +32,157 @@ def tile_corrlosschamfer_kernel(tc, verts, cams, offs, out):
     with (
         tc.tile_pool(name="held", bufs=1) as held,
         tc.tile_pool(name="work", bufs=len(PIECES)) as work,
-        tc.psum_pool(name="spread_out", bufs=1) as spread_out,
+        tc.psum_pool(name="moved", bufs=1) as moved,
         tc.psum_pool(name="sums", bufs=3) as sums,
     ):
-        cam = held.tile([SAMPLES, 7], F32, name="cam")
-        nc.sync.dma_start(cam[:], cams)
+        verts_of = verts.rearrange("(k q i h) c -> k h q i c", k=3, q=2, h=2)
+        cam_rows = held.tile([SAMPLES, 7], F32, name="cam_rows")
+        nc.sync.dma_start(cam_rows[:], cams)
         windows = [held.tile([128, VERTICES], F32, name=f"window{t}") for t in range(3)]
         offsets = held.tile([128, PICKS // 16], U16, name="offsets")
-
-        def load_window(t):
-            for first, count in ((0, 2), (2, 1), (3, 1)):
-                k, group = WINDOWS[t][first]
-                row = k * SAMPLES + group * GROUP
-                nc.sync.dma_start(
-                    windows[t][first * GROUP : (first + count) * GROUP, :],
-                    verts[row : row + count * GROUP, :],
-                )
-
-        load_window(0)
-        nc.sync.dma_start(offsets[:], offs)
-        load_window(1)
-        load_window(2)
+        for t in range(3):
+            for j in range(BLOCKS):
+                k, s = WINDOWS[t][j]
+                nc.sync.dma_start(windows[t][j::BLOCKS, :], verts_of[k, s // 2, s % 2])
+            if t == 0:
+                nc.sync.dma_start(offsets[:], offs)
         shift = held.tile([128, 2], F32, name="shift")
         for r in range(2):
             nc.sync.dma_start(
-                shift[64 * r : 64 * (r + 1), :],
-                cams.rearrange("(h p) c -> p h c", h=2)[:, :, 1 + r],
+                shift[64 * r : 64 * (r + 1), :], cams.rearrange("(m h) c -> m h c", h=2)[:, :, 1 + r]
             )
-        scale = cam[:, 0:1]
-        quat = cam[:, 3:7]
 
-        identity = held.tile([SAMPLES, SAMPLES], F32, name="identity")
+        identity = held.tile([128, 128], F32, name="identity")
         make_identity(nc, identity[:])
-        half = held.tile([SAMPLES, 1], F32, name="half")
-        nc.gpsimd.memset(half[:], 0.5)
-        diagonal_eps = held.tile([SAMPLES, 6], F32, name="diagonal_eps")
-        nc.gpsimd.memset(diagonal_eps[:], 0.0)
-        nc.gpsimd.memset(diagonal_eps[:, 0:4:3], EPS)
-        rootless_tile = held.tile([SAMPLES, 9], F32, name="rootless_tile")
-        nc.gpsimd.memset(rootless_tile[:], TINY)
-        rootless_and_floor = rootless_tile[:].rearrange("p (k c) -> p k c", c=3)
-        rootless = rootless_and_floor[:, :, 0:2]
+        by_block = identity[:].rearrange("p (i j) -> p i j", j=BLOCKS)
+        root = held.tile([128, 3], F32, name="root")
+        nc.gpsimd.memset(root[:], 0.5)
+        own_tile = held.tile([128, 3, 3], F32, name="own_tile")
+        nc.gpsimd.memset(own_tile[:], TINY)
+        own = own_tile[:, :, 0:2]
         ones = held.tile([128, WIDEST], F32, name="ones")
         nc.gpsimd.memset(ones[:], 1.0)
+        def blocks_of(t, belongs):
+            js = [j for j in range(BLOCKS) if belongs(WINDOWS[t][j])]
+            return slice(js[0], js[-1] + 1, js[1] - js[0] if len(js) > 1 else 1)
+
+        by_sample = identity[:].rearrange("b (q i h) -> b h q i", q=2, h=2)
+        placed = []
+        for t in range(3):
+            placed.append(held.tile([SAMPLES, GROUP, BLOCKS], F32, name=f"placed{t}"))
+            for s in sorted({s for k, s in WINDOWS[t]}):
+                into = placed[t][:, :, blocks_of(t, lambda block: block[1] == s)]
+                nc.vector.tensor_copy(into, by_sample[:, s // 2, s % 2].unsqueeze(2).to_broadcast(into.shape))
+        block = held.tile([128, BLOCKS], F32, name="block")
+        nc.vector.tensor_reduce(block[:], identity[:].rearrange("p (i j) -> p j i", j=BLOCKS), axis=X, op=ALU.add)
+        coordinate = held.tile([128, 9], F32, name="coordinate")
+        by_coordinate = coordinate[:].rearrange("p (t k) -> p t k", k=3)
+        nc.vector.tensor_copy(by_coordinate, block[:, 0:3].unsqueeze(1).to_broadcast([128, 3, 3]))
+        nc.vector.tensor_scalar(coordinate[:, 0:9:4], coordinate[:, 0:9:4], block[:, 3:4], None, ALU.add)
         pattern = []
         for t in range(3):
             pattern.append(held.tile([128, 2, GROUP], F32, name=f"pattern{t}"))
-            nc.vector.memset(pattern[t][:], 0.0)
-            for j in range(4):
-                block = slice(j * GROUP, (j + 1) * GROUP)
-                nc.vector.tensor_copy(pattern[t][block, WINDOWS[t][j][1] % 2, :], identity[block, block])
+            for q in range(2):
+                js = blocks_of(t, lambda block: block[1] % 2 == q)
+                nc.vector.tensor_reduce(pattern[t][:, q, :], by_block[:, :, js], axis=X, op=ALU.add)
 
-        def by_k(six):
-            return six[:].rearrange("p (k r) -> p k r", r=2)
-
-        pair = held.tile([SAMPLES, 16], F32, name="pair")
+        cam_moved = moved.tile([128, 3, 7], F32, name="cam_moved")
+        for t in range(3):
+            nc.tensor.matmul(
+                cam_moved[:, t, :], placed[t][:].rearrange("b i j -> b (i j)"), cam_rows[:], start=True, stop=True
+            )
+        cam = held.tile([128, 3, 7], F32, name="cam")
+        nc.vector.tensor_copy(cam[:], cam_moved[:])
+        scale = cam[:, :, 0]
+        quat = cam[:, :, 3:7]
+        pair = held.tile([128, 3, 16], F32, name="pair")
         nc.vector.tensor_tensor(
-            pair[:].rearrange("p (i j) -> p i j", i=4),
-            quat.unsqueeze(2).to_broadcast([SAMPLES, 4, 4]),
-            quat.unsqueeze(1).to_broadcast([SAMPLES, 4, 4]),
+            pair[:].rearrange("p t (i j) -> p t i j", i=4),
+            quat.unsqueeze(3).to_broadcast([128, 3, 4, 4]),
+            quat.unsqueeze(2).to_broadcast([128, 3, 4, 4]),
             ALU.mult,
         )
-        sumsq = held.tile([SAMPLES, 1], F32, name="sumsq")
-        nc.vector.reduce_sum(sumsq[:], pair[:, 0:16:5], axis=mybir.AxisListType.X)
-        norm = held.tile([SAMPLES, 1], F32, name="norm")
-        nc.gpsimd.tensor_tensor(norm[:], sumsq[:], half[:], ALU.pow)
+        sumsq = held.tile([128, 3], F32, name="sumsq")
+        nc.vector.reduce_sum(sumsq[:], pair[:, :, 0:16:5], axis=X)
+        norm = held.tile([128, 3], F32, name="norm")
+        nc.gpsimd.tensor_tensor(norm[:], sumsq[:], root[:], ALU.pow)
 
         def pr(i, j):
             return 4 * i + j
 
-        def mixed(r, k):
-            return 3 * k + r
-
+        mixed = held.tile([128, 3, 6], F32, name="mixed")
         nc.vector.tensor_tensor(
-            rootless_tile[:, mixed(1, 0) : mixed(0, 2) + 1 : 5],
-            pair[:, pr(QX, QY) : pr(QX, QZ) + 1],
-            pair[:, pr(QY, QW) : pr(QZ, QW) + 1 : 4][:, ::-1],
+            mixed[:, :, 2:4],
+            pair[:, :, pr(QX, QY) : pr(QX, QZ) + 1][:, :, ::-1],
+            pair[:, :, pr(QY, QW) : pr(QZ, QW) + 1 : 4],
             ALU.add,
         )
         nc.vector.tensor_tensor(
-            rootless_tile[:, mixed(0, 1) : mixed(1, 2) + 1 : 4],
-            pair[:, pr(QX, QY) : pr(QY, QZ) + 1 : 5],
-            pair[:, pr(QW, QX) : pr(QW, QZ) + 1 : 2][:, ::-1],
+            mixed[:, :, 1:6:4],
+            pair[:, :, pr(QX, QY) : pr(QY, QZ) + 1 : 5],
+            pair[:, :, pr(QW, QX) : pr(QW, QZ) + 1 : 2][:, :, ::-1],
             ALU.subtract,
         )
-        base = held.tile([SAMPLES, 1], F32, name="base")
+        base = held.tile([128, 3], F32, name="base")
         nc.vector.tensor_scalar(base[:], sumsq[:], 0.5, 0.5 * EPS * EPS, ALU.mult, ALU.add)
-        squares = held.tile([SAMPLES, 2], F32, name="squares")
-        nc.vector.tensor_scalar(
-            squares[:], pair[:, pr(QX, QX) : pr(QY, QY) + 1 : 5], pair[:, pr(QZ, QZ) : pr(QZ, QZ) + 1], None, ALU.add
+        squares = held.tile([128, 3, 2], F32, name="squares")
+        nc.vector.tensor_tensor(
+            squares[:],
+            pair[:, :, pr(QX, QX) : pr(QY, QY) + 1 : 5][:, :, ::-1],
+            pair[:, :, pr(QZ, QZ) : pr(QZ, QZ) + 1].to_broadcast([128, 3, 2]),
+            ALU.add,
         )
-        nc.vector.tensor_scalar(
-            rootless_tile[:, mixed(0, 0) : mixed(1, 1) + 1 : 4], squares[:, ::-1], -1.0, base[:, 0:1], ALU.mult, ALU.add
+        nc.vector.tensor_tensor(
+            mixed[:, :, 0:5:4], base[:].unsqueeze(2).to_broadcast([128, 3, 2]), squares[:], ALU.subtract
         )
-        larger = held.tile([SAMPLES, 3], F32, name="larger")
-        nc.vector.tensor_reduce(
-            larger[:], rootless_and_floor, axis=mybir.AxisListType.X, op=ALU.max, apply_absolute_value=True
+        masked = held.tile([128, 3, 2, 3], F32, name="masked")
+        nc.vector.tensor_tensor(
+            masked[:],
+            mixed[:].rearrange("p t (r k) -> p t r k", k=3),
+            by_coordinate.unsqueeze(2).to_broadcast([128, 3, 2, 3]),
+            ALU.mult,
         )
-        inv_base = held.tile([SAMPLES, 1], F32, name="inv_base")
+        nc.vector.tensor_reduce(own, masked[:], axis=X, op=ALU.add)
+        larger = held.tile([128, 3], F32, name="larger")
+        nc.vector.tensor_reduce(larger[:], own_tile[:], axis=X, op=ALU.max, apply_absolute_value=True)
+        inv_base = held.tile([128, 3], F32, name="inv_base")
         nc.vector.reciprocal(inv_base[:], base[:])
-        pivots = held.tile([SAMPLES, 3], F32, name="pivots")
-        nc.vector.tensor_scalar(pivots[:], larger[:], inv_base[:, 0:1], None, ALU.mult)
-
-        def to_windows(dest, source, columns):
-            for t in range(3):
-                for j in range(4):
-                    k, group = WINDOWS[t][j]
-                    nc.tensor.matmul(
-                        dest[j * GROUP : (j + 1) * GROUP, t, :],
-                        identity[:, group * GROUP : (group + 1) * GROUP],
-                        source[:, columns * k : columns * (k + 1)],
-                        start=True,
-                        stop=True,
-                    )
-
-        pivot = spread_out.tile([128, 3, 1], F32, name="pivot")
-        to_windows(pivot, pivots, 1)
         spread = [held.tile([128, WIDEST], F32, name=f"spread{t}") for t in range(3)]
-        nc.vector.tensor_scalar(spread[0][:], ones[:], pivot[:, 0, :], None, ALU.mult)
+        nc.vector.tensor_scalar(spread[0][:], ones[:], larger[:, 0:1], inv_base[:, 0:1], ALU.mult, ALU.mult)
         for t in (1, 2):
-            nc.scalar.activation(spread[t][:], pivot[:, t, :].to_broadcast([128, WIDEST]), ACT.Identity)
+            nc.scalar.activation(
+                spread[t][:], larger[:, t : t + 1].to_broadcast([128, WIDEST]), ACT.Identity, scale=inv_base[:, t : t + 1]
+            )
 
-        inv_larger = held.tile([SAMPLES, 3], F32, name="inv_larger")
+        inv_larger = held.tile([128, 3], F32, name="inv_larger")
         nc.vector.reciprocal(inv_larger[:], larger[:])
-        scale_by_pivot = held.tile([SAMPLES, 3], F32, name="scale_by_pivot")
-        nc.vector.tensor_scalar(scale_by_pivot[:], inv_larger[:], scale, base[:, 0:1], ALU.mult, ALU.mult)
-        numer = held.tile([SAMPLES, 6], F32, name="numer")
-        nc.vector.scalar_tensor_tensor(by_k(numer), by_k(diagonal_eps), norm[:, 0:1], rootless, ALU.mult, ALU.add)
-        halved = held.tile([SAMPLES, 1], F32, name="halved")
-        nc.vector.scalar_tensor_tensor(halved[:], norm[:], EPS, base[:], ALU.mult, ALU.add)
-        inv_halved = held.tile([SAMPLES, 1], F32, name="inv_halved")
-        nc.vector.reciprocal(inv_halved[:], halved[:])
-        factors = held.tile([SAMPLES, 6], F32, name="factors")
-        nc.vector.scalar_tensor_tensor(
-            by_k(factors),
-            by_k(numer),
-            inv_halved[:, 0:1],
-            scale_by_pivot[:].unsqueeze(2).to_broadcast([SAMPLES, 3, 2]),
-            ALU.mult,
-            ALU.mult,
+        scaled = held.tile([128, 3], F32, name="scaled")
+        nc.vector.tensor_tensor(scaled[:], scale, base[:], ALU.mult)
+        scale_by_pivot = held.tile([128, 3], F32, name="scale_by_pivot")
+        nc.vector.tensor_tensor(scale_by_pivot[:], scaled[:], inv_larger[:], ALU.mult)
+        on_diagonal = held.tile([128, 3, 2], F32, name="on_diagonal")
+        nc.vector.tensor_tensor(
+            on_diagonal[:], by_coordinate[:, :, 0:2], norm[:].unsqueeze(2).to_broadcast([128, 3, 2]), ALU.mult
         )
-        factor_psum = spread_out.tile([128, 3, 2], F32, name="factor_psum")
-        to_windows(factor_psum, factors, 2)
+        numer = held.tile([128, 3, 2], F32, name="numer")
+        nc.vector.scalar_tensor_tensor(numer[:], on_diagonal[:], EPS, own, ALU.mult, ALU.add)
+        halved = held.tile([128, 3], F32, name="halved")
+        nc.vector.scalar_tensor_tensor(halved[:], norm[:], EPS, base[:], ALU.mult, ALU.add)
+        inv_halved = held.tile([128, 3], F32, name="inv_halved")
+        nc.vector.reciprocal(inv_halved[:], halved[:])
+        gain = held.tile([128, 3], F32, name="gain")
+        nc.vector.tensor_tensor(gain[:], scale_by_pivot[:], inv_halved[:], ALU.mult)
         factor = held.tile([128, 3, 2], F32, name="factor")
-        nc.scalar.activation(factor[:], factor_psum[:], ACT.Identity)
+        nc.vector.tensor_tensor(factor[:], numer[:], gain[:].unsqueeze(2).to_broadcast([128, 3, 2]), ALU.mult)
         weights = []
         for t in range(3):
             weights.append(held.tile([128, 2, 2, GROUP], F32, name=f"weights{t}"))
             for r in range(2):
                 nc.scalar.activation(weights[t][:, r, :, :], pattern[t][:], ACT.Identity, scale=factor[:, t, r : r + 1])
 
-        out_u_v = out.rearrange("(r h p) c -> r p h c", r=2, h=2)
+        out_of = out.rearrange("(m h) c -> m h c", h=2)
         first = 0
         for width in PIECES:
-            columns = slice(first, first + width)
             piece_offsets = offsets[:, first // 16 : (first + width) // 16]
             total = [sums.tile([128, width], F32, name=f"total{h}") for h in range(2)]
             for t in range(3):
@@ -193,19 +190,19 @@ def tile_corrlosschamfer_kernel(tc, verts, cams, offs, out):
                 nc.vector.tensor_tensor(
                     picked[:], windows[t][:].indirect(piece_offsets), spread[t][:, 0:width], ALU.mult
                 )
-                for group in sorted({g for k, g in WINDOWS[t]}):
+                for s in sorted({s for k, s in WINDOWS[t]}):
+                    h, q = s // 2, s % 2
                     for r in range(2):
-                        quadrant = 2 * r + group % 2
+                        quadrant = 2 * r + q
                         nc.tensor.matmul(
-                            total[group // 2][quadrant * GROUP : (quadrant + 1) * GROUP, :],
-                            weights[t][:, r, group % 2, :],
+                            total[h][quadrant * GROUP : (quadrant + 1) * GROUP, :],
+                            weights[t][:, r, q, :],
                             picked[:],
-                            start=(t == windows_of(group)[0]),
-                            stop=(t == windows_of(group)[-1]),
+                            start=(t == FIRST_WINDOW[s]),
+                            stop=(t == LAST_WINDOW[s]),
                         )
             image = work.tile([128, 2, width], F32, name="image")
             for h in range(2):
                 nc.scalar.activation(image[:, h, :], total[h][:], ACT.Identity, bias=shift[:, h : h + 1])
-            for r in range(2):
-                nc.sync.dma_start(out_u_v[r][:, :, columns], image[64 * r : 64 * (r + 1), :, :])
+            nc.sync.dma_start(out_of[:, :, first : first + width], image[:])
             first += width

@@ -12,7 +12,7 @@ GROUP = 32
 BLOCKS = 4
 VERTICES = 2048
 PICKS = 2048
-PIECES = (128, 384, 512, 512, 384, 128)
+PIECES = (512, 512, 512, 384, 128)
 WIDEST = max(PIECES)
 assert sum(PIECES) == PICKS and all(width % 32 == 0 for width in PIECES)
 EPS = 1e-8
@@ -23,17 +23,20 @@ WINDOWS = (
     ((0, 2), (1, 1), (2, 1), (1, 2)),
     ((0, 3), (1, 3), (2, 3), (2, 2)),
 )
+GROUPS_OF = ((0, 1), (2, 1), (3, 2))
 FIRST_WINDOW = {0: 0, 1: 0, 2: 1, 3: 2}
 LAST_WINDOW = {0: 0, 1: 1, 2: 2, 3: 2}
+BANK_OPENS = {0: 0, 1: 1}
+BANK_CLOSES = {0: 1, 1: 2}
 
 
 def tile_corrlosschamfer_kernel(tc, verts, cams, offs, out):
     nc = tc.nc
     with (
         tc.tile_pool(name="held", bufs=1) as held,
-        tc.tile_pool(name="work", bufs=len(PIECES)) as work,
-        tc.psum_pool(name="moved", bufs=1) as moved,
-        tc.psum_pool(name="sums", bufs=3) as sums,
+        tc.tile_pool(name="work", bufs=3 * len(PIECES)) as work,
+        tc.tile_pool(name="images", bufs=len(PIECES)) as images,
+        tc.psum_pool(name="sums", bufs=8) as sums,
     ):
         verts_of = verts.rearrange("(k q i h) c -> k h q i c", k=3, q=2, h=2)
         cam_rows = held.tile([SAMPLES, 7], F32, name="cam_rows")
@@ -46,163 +49,180 @@ def tile_corrlosschamfer_kernel(tc, verts, cams, offs, out):
                 nc.sync.dma_start(windows[t][j::BLOCKS, :], verts_of[k, s // 2, s % 2])
             if t == 0:
                 nc.sync.dma_start(offsets[:], offs)
-        shift = held.tile([128, 2], F32, name="shift")
-        for r in range(2):
-            nc.sync.dma_start(
-                shift[64 * r : 64 * (r + 1), :], cams.rearrange("(m h) c -> m h c", h=2)[:, :, 1 + r]
-            )
+        quat = cam_rows[:, 3:7]
+        scale = cam_rows[:, 0:1]
+        quat = cam_rows[:, 3:7]
 
         identity = held.tile([128, 128], F32, name="identity")
         make_identity(nc, identity[:])
         by_block = identity[:].rearrange("p (i j) -> p i j", j=BLOCKS)
-        root = held.tile([128, 3], F32, name="root")
-        nc.gpsimd.memset(root[:], 0.5)
-        own_tile = held.tile([128, 3, 3], F32, name="own_tile")
-        nc.gpsimd.memset(own_tile[:], TINY)
-        own = own_tile[:, :, 0:2]
-        ones = held.tile([128, WIDEST], F32, name="ones")
-        nc.gpsimd.memset(ones[:], 1.0)
-        def blocks_of(t, belongs):
-            js = [j for j in range(BLOCKS) if belongs(WINDOWS[t][j])]
-            return slice(js[0], js[-1] + 1, js[1] - js[0] if len(js) > 1 else 1)
-
         by_sample = identity[:].rearrange("b (q i h) -> b h q i", q=2, h=2)
-        placed = []
-        for t in range(3):
-            placed.append(held.tile([SAMPLES, GROUP, BLOCKS], F32, name=f"placed{t}"))
-            for s in sorted({s for k, s in WINDOWS[t]}):
-                into = placed[t][:, :, blocks_of(t, lambda block: block[1] == s)]
-                nc.vector.tensor_copy(into, by_sample[:, s // 2, s % 2].unsqueeze(2).to_broadcast(into.shape))
+        placed = [held.tile([SAMPLES, GROUP, BLOCKS], F32, name=f"placed{t}") for t in range(3)]
+
+        def place(t):
+            for s in GROUPS_OF[t]:
+                js = [j for j in range(BLOCKS) if WINDOWS[t][j][1] == s]
+                into = placed[t][:, :, js[0] : js[-1] + 1 : max(1, js[-1] - js[0] - len(js) + 2)]
+                nc.gpsimd.tensor_copy(into, by_sample[:, s // 2, s % 2].unsqueeze(2).to_broadcast(into.shape))
+
+        three_one = held.tile([128, 2, GROUP], F32, name="three_one")
+        two_two = held.tile([128, 2, GROUP], F32, name="two_two")
+        pattern = (three_one, two_two, three_one)
+        place(0)
+        nc.gpsimd.tensor_tensor(two_two[:, 1, :], by_block[:, :, 1], by_block[:, :, 2], ALU.add)
+        nc.gpsimd.tensor_tensor(three_one[:, 0, :], two_two[:, 1, :], by_block[:, :, 0], ALU.add)
+        nc.gpsimd.tensor_copy(three_one[:, 1, :], by_block[:, :, 3])
+        place(1)
+        place(2)
+        nc.gpsimd.tensor_tensor(two_two[:, 0, :], by_block[:, :, 0], by_block[:, :, 3], ALU.add)
+        tiny = held.tile([SAMPLES, 1], F32, name="tiny")
+        nc.vector.memset(tiny[:], TINY)
+        early_root = held.tile([SAMPLES, 1], F32, name="early_root")
+        nc.scalar.activation(early_root[:], tiny[:], ACT.Sqrt)
+        ones = held.tile([128, WIDEST], F32, name="ones")
+        nc.vector.memset(ones[:], 1.0)
+        diagonal = held.tile([SAMPLES, 6], F32, name="diagonal")
+        nc.vector.memset(diagonal[:], 0.0)
+        nc.vector.memset(diagonal[:, 0:5:4], 1.0)
+        masked = held.tile([128, 3, 7], F32, name="masked")
+        nc.vector.memset(masked[:], TINY)
         block = held.tile([128, BLOCKS], F32, name="block")
         nc.vector.tensor_reduce(block[:], identity[:].rearrange("p (i j) -> p j i", j=BLOCKS), axis=X, op=ALU.add)
         coordinate = held.tile([128, 9], F32, name="coordinate")
         by_coordinate = coordinate[:].rearrange("p (t k) -> p t k", k=3)
         nc.vector.tensor_copy(by_coordinate, block[:, 0:3].unsqueeze(1).to_broadcast([128, 3, 3]))
         nc.vector.tensor_scalar(coordinate[:, 0:9:4], coordinate[:, 0:9:4], block[:, 3:4], None, ALU.add)
-        pattern = []
-        for t in range(3):
-            pattern.append(held.tile([128, 2, GROUP], F32, name=f"pattern{t}"))
-            for q in range(2):
-                js = blocks_of(t, lambda block: block[1] % 2 == q)
-                nc.vector.tensor_reduce(pattern[t][:, q, :], by_block[:, :, js], axis=X, op=ALU.add)
 
-        cam_moved = moved.tile([128, 3, 7], F32, name="cam_moved")
-        for t in range(3):
-            nc.tensor.matmul(
-                cam_moved[:, t, :], placed[t][:].rearrange("b i j -> b (i j)"), cam_rows[:], start=True, stop=True
-            )
-        cam = held.tile([128, 3, 7], F32, name="cam")
-        nc.vector.tensor_copy(cam[:], cam_moved[:])
-        scale = cam[:, :, 0]
-        quat = cam[:, :, 3:7]
-        pair = held.tile([128, 3, 16], F32, name="pair")
+        sumsq = held.tile([SAMPLES, 1], F32, name="sumsq")
+        square = held.tile([SAMPLES, 4], F32, name="square")
+        nc.scalar.activation(square[:], quat, ACT.Square, accum_out=sumsq[:])
+        norm = held.tile([SAMPLES, 1], F32, name="norm")
+        nc.scalar.activation(norm[:], sumsq[:], ACT.Sqrt, bias=tiny[:])
+        pair = held.tile([SAMPLES, 16], F32, name="pair")
         nc.vector.tensor_tensor(
-            pair[:].rearrange("p t (i j) -> p t i j", i=4),
-            quat.unsqueeze(3).to_broadcast([128, 3, 4, 4]),
-            quat.unsqueeze(2).to_broadcast([128, 3, 4, 4]),
+            pair[:].rearrange("p (i j) -> p i j", i=4),
+            quat.unsqueeze(2).to_broadcast([SAMPLES, 4, 4]),
+            quat.unsqueeze(1).to_broadcast([SAMPLES, 4, 4]),
             ALU.mult,
         )
-        sumsq = held.tile([128, 3], F32, name="sumsq")
-        nc.vector.reduce_sum(sumsq[:], pair[:, :, 0:16:5], axis=X)
-        norm = held.tile([128, 3], F32, name="norm")
-        nc.gpsimd.tensor_tensor(norm[:], sumsq[:], root[:], ALU.pow)
 
         def pr(i, j):
             return 4 * i + j
 
-        mixed = held.tile([128, 3, 6], F32, name="mixed")
+        mixed = held.tile([SAMPLES, 6], F32, name="mixed")
         nc.vector.tensor_tensor(
-            mixed[:, :, 2:4],
-            pair[:, :, pr(QX, QY) : pr(QX, QZ) + 1][:, :, ::-1],
-            pair[:, :, pr(QY, QW) : pr(QZ, QW) + 1 : 4],
+            mixed[:, 2:4],
+            pair[:, pr(QX, QY) : pr(QX, QZ) + 1][:, ::-1],
+            pair[:, pr(QY, QW) : pr(QZ, QW) + 1 : 4],
             ALU.add,
         )
         nc.vector.tensor_tensor(
-            mixed[:, :, 1:6:4],
-            pair[:, :, pr(QX, QY) : pr(QY, QZ) + 1 : 5],
-            pair[:, :, pr(QW, QX) : pr(QW, QZ) + 1 : 2][:, :, ::-1],
+            mixed[:, 1:6:4],
+            pair[:, pr(QX, QY) : pr(QY, QZ) + 1 : 5],
+            pair[:, pr(QW, QX) : pr(QW, QZ) + 1 : 2][:, ::-1],
             ALU.subtract,
         )
-        base = held.tile([128, 3], F32, name="base")
-        nc.vector.tensor_scalar(base[:], sumsq[:], 0.5, 0.5 * EPS * EPS, ALU.mult, ALU.add)
-        squares = held.tile([128, 3, 2], F32, name="squares")
-        nc.vector.tensor_tensor(
-            squares[:],
-            pair[:, :, pr(QX, QX) : pr(QY, QY) + 1 : 5][:, :, ::-1],
-            pair[:, :, pr(QZ, QZ) : pr(QZ, QZ) + 1].to_broadcast([128, 3, 2]),
+        nc.vector.tensor_scalar(
+            mixed[:, 0:5:4],
+            pair[:, pr(QX, QX) : pr(QY, QY) + 1 : 5][:, ::-1],
+            pair[:, pr(QZ, QZ) : pr(QZ, QZ) + 1],
+            -1.0,
             ALU.add,
+            ALU.mult,
         )
+        base = held.tile([SAMPLES, 1], F32, name="base")
+        nc.vector.tensor_scalar(base[:], sumsq[:], 0.5, 0.5 * EPS * EPS, ALU.mult, ALU.add)
+        halved = held.tile([SAMPLES, 1], F32, name="halved")
+        nc.vector.scalar_tensor_tensor(halved[:], norm[:], EPS, base[:], ALU.mult, ALU.add)
+        numer = held.tile([SAMPLES, 6], F32, name="numer")
+        nc.vector.scalar_tensor_tensor(numer[:], diagonal[:], halved[:, 0:1], mixed[:], ALU.mult, ALU.add)
+
+        moved = sums.tile([128, 3, 6], F32, name="moved", tag="bank")
+        for t in range(3):
+            nc.tensor.matmul(
+                moved[:, t, :], placed[t][:].rearrange("b i j -> b (i j)"), numer[:], start=True, stop=True
+            )
+        by_rk = masked[:, :, 0:6].rearrange("p t (r k) -> p t r k", k=3)
         nc.vector.tensor_tensor(
-            mixed[:, :, 0:5:4], base[:].unsqueeze(2).to_broadcast([128, 3, 2]), squares[:], ALU.subtract
-        )
-        masked = held.tile([128, 3, 2, 3], F32, name="masked")
-        nc.vector.tensor_tensor(
-            masked[:],
-            mixed[:].rearrange("p t (r k) -> p t r k", k=3),
+            by_rk,
+            moved[:].rearrange("p t (r k) -> p t r k", k=3),
             by_coordinate.unsqueeze(2).to_broadcast([128, 3, 2, 3]),
             ALU.mult,
         )
-        nc.vector.tensor_reduce(own, masked[:], axis=X, op=ALU.add)
-        larger = held.tile([128, 3], F32, name="larger")
-        nc.vector.tensor_reduce(larger[:], own_tile[:], axis=X, op=ALU.max, apply_absolute_value=True)
-        inv_base = held.tile([128, 3], F32, name="inv_base")
-        nc.vector.reciprocal(inv_base[:], base[:])
-        spread = [held.tile([128, WIDEST], F32, name=f"spread{t}") for t in range(3)]
-        nc.vector.tensor_scalar(spread[0][:], ones[:], larger[:, 0:1], inv_base[:, 0:1], ALU.mult, ALU.mult)
-        for t in (1, 2):
-            nc.scalar.activation(
-                spread[t][:], larger[:, t : t + 1].to_broadcast([128, WIDEST]), ACT.Identity, scale=inv_base[:, t : t + 1]
-            )
+        pivot = held.tile([128, 3], F32, name="pivot")
+        nc.vector.tensor_reduce(pivot[:], masked[:], axis=X, op=ALU.max, apply_absolute_value=True)
 
-        inv_larger = held.tile([128, 3], F32, name="inv_larger")
-        nc.vector.reciprocal(inv_larger[:], larger[:])
-        scaled = held.tile([128, 3], F32, name="scaled")
-        nc.vector.tensor_tensor(scaled[:], scale, base[:], ALU.mult)
-        scale_by_pivot = held.tile([128, 3], F32, name="scale_by_pivot")
-        nc.vector.tensor_tensor(scale_by_pivot[:], scaled[:], inv_larger[:], ALU.mult)
-        on_diagonal = held.tile([128, 3, 2], F32, name="on_diagonal")
-        nc.vector.tensor_tensor(
-            on_diagonal[:], by_coordinate[:, :, 0:2], norm[:].unsqueeze(2).to_broadcast([128, 3, 2]), ALU.mult
-        )
-        numer = held.tile([128, 3, 2], F32, name="numer")
-        nc.vector.scalar_tensor_tensor(numer[:], on_diagonal[:], EPS, own, ALU.mult, ALU.add)
-        halved = held.tile([128, 3], F32, name="halved")
-        nc.vector.scalar_tensor_tensor(halved[:], norm[:], EPS, base[:], ALU.mult, ALU.add)
-        inv_halved = held.tile([128, 3], F32, name="inv_halved")
-        nc.vector.reciprocal(inv_halved[:], halved[:])
-        gain = held.tile([128, 3], F32, name="gain")
-        nc.vector.tensor_tensor(gain[:], scale_by_pivot[:], inv_halved[:], ALU.mult)
+        own = held.tile([128, 3, 2], F32, name="own")
+        nc.vector.tensor_reduce(own[:], by_rk, axis=X, op=ALU.add)
+        inv_pivot = held.tile([128, 3], F32, name="inv_pivot")
+        nc.vector.reciprocal(inv_pivot[:], pivot[:])
         factor = held.tile([128, 3, 2], F32, name="factor")
-        nc.vector.tensor_tensor(factor[:], numer[:], gain[:].unsqueeze(2).to_broadcast([128, 3, 2]), ALU.mult)
-        weights = []
-        for t in range(3):
-            weights.append(held.tile([128, 2, 2, GROUP], F32, name=f"weights{t}"))
+        nc.vector.tensor_tensor(factor[:], own[:], inv_pivot[:].unsqueeze(2).to_broadcast([128, 3, 2]), ALU.mult)
+        weights = [held.tile([128, 2, 2, GROUP], F32, name=f"weights{t}") for t in range(3)]
+        nc.vector.scalar_tensor_tensor(
+            weights[0][:].rearrange("p r g i -> p r (g i)"),
+            pattern[0][:].rearrange("p g i -> p (g i)").unsqueeze(1).to_broadcast([128, 2, 2 * GROUP]),
+            inv_pivot[:, 0:1],
+            own[:, 0, :].unsqueeze(2).to_broadcast([128, 2, 2 * GROUP]),
+            ALU.mult,
+            ALU.mult,
+        )
+        spread = [held.tile([128, WIDEST], F32, name=f"spread{t}") for t in range(3)]
+        nc.vector.tensor_scalar(spread[0][:], ones[:], pivot[:, 0:1], None, ALU.mult)
+        for t in (1, 2):
+            nc.scalar.activation(spread[t][:], pivot[:, t : t + 1].to_broadcast([128, WIDEST]), ACT.Identity)
             for r in range(2):
                 nc.scalar.activation(weights[t][:, r, :, :], pattern[t][:], ACT.Identity, scale=factor[:, t, r : r + 1])
 
+        finish = held.tile([SAMPLES, 4], F32, name="finish")
+        nc.scalar.activation(finish[:, 0:4:2], cam_rows[:, 1:3], ACT.Identity)
+        inv_halved = held.tile([SAMPLES, 1], F32, name="inv_halved")
+        nc.vector.reciprocal(inv_halved[:], halved[:])
+        nc.vector.tensor_scalar(finish[:, 1:4:2], inv_halved[:].to_broadcast([SAMPLES, 2]), scale, None, ALU.mult)
+        moved_finish = sums.tile([128, 2, 2], F32, name="moved_finish", tag="bank")
+        for h in range(2):
+            for r in range(2):
+                for q in range(2):
+                    quadrant = 2 * r + q
+                    nc.tensor.matmul(
+                        moved_finish[quadrant * GROUP : (quadrant + 1) * GROUP, h, :],
+                        by_sample[:, h, q],
+                        finish[:, 2 * r : 2 * r + 2],
+                        start=True,
+                        stop=True,
+                    )
+        bank_finish = held.tile([128, 2, 2], F32, name="bank_finish")
+        nc.scalar.activation(bank_finish[:], moved_finish[:], ACT.Identity)
+
         out_of = out.rearrange("(m h) c -> m h c", h=2)
-        first = 0
-        for width in PIECES:
-            piece_offsets = offsets[:, first // 16 : (first + width) // 16]
-            total = [sums.tile([128, width], F32, name=f"total{h}") for h in range(2)]
-            for t in range(3):
-                picked = work.tile([128, width], F32, name=f"picked{t}")
+        starts = [sum(PIECES[:n]) for n in range(len(PIECES))]
+        total = {}
+        for t in range(3):
+            for n, width in enumerate(PIECES):
+                columns = slice(starts[n], starts[n] + width)
+                picked = work.tile([128, width], F32, name="picked")
                 nc.vector.tensor_tensor(
-                    picked[:], windows[t][:].indirect(piece_offsets), spread[t][:, 0:width], ALU.mult
+                    picked[:],
+                    windows[t][:].indirect(offsets[:, starts[n] // 16 : (starts[n] + width) // 16]),
+                    spread[t][:, 0:width],
+                    ALU.mult,
                 )
-                for s in sorted({s for k, s in WINDOWS[t]}):
+                for h in range(2):
+                    if BANK_OPENS[h] == t:
+                        total[n, h] = sums.tile([128, width], F32, name=f"total{h}", tag="bank")
+                for g, s in enumerate(GROUPS_OF[t]):
                     h, q = s // 2, s % 2
                     for r in range(2):
                         quadrant = 2 * r + q
                         nc.tensor.matmul(
-                            total[h][quadrant * GROUP : (quadrant + 1) * GROUP, :],
-                            weights[t][:, r, q, :],
+                            total[n, h][quadrant * GROUP : (quadrant + 1) * GROUP, :],
+                            weights[t][:, r, g, :],
                             picked[:],
                             start=(t == FIRST_WINDOW[s]),
                             stop=(t == LAST_WINDOW[s]),
                         )
-            image = work.tile([128, 2, width], F32, name="image")
-            for h in range(2):
-                nc.scalar.activation(image[:, h, :], total[h][:], ACT.Identity, bias=shift[:, h : h + 1])
-            nc.sync.dma_start(out_of[:, :, first : first + width], image[:])
-            first += width
+                for h in range(2):
+                    if BANK_CLOSES[h] == t:
+                        image = images.tile([128, width], F32, name=f"image{h}")
+                        nc.scalar.activation(image[:], total[n, h][:], ACT.Identity, bias=bank_finish[:, h, 0:1], scale=bank_finish[:, h, 1:2])
+                        nc.sync.dma_start(out_of[:, h, columns], image[:])

import concourse.mybir as mybir
from concourse.masks import make_identity

F32 = mybir.dt.float32
U16 = mybir.dt.uint16
ALU = mybir.AluOpType
ACT = mybir.ActivationFunctionType
X = mybir.AxisListType.X

SAMPLES = 128
GROUP = 32
BLOCKS = 4
VERTICES = 2048
PICKS = 2048
PIECES = (512, 512, 512, 384, 128)
WIDEST = max(PIECES)
assert sum(PIECES) == PICKS and all(width % 32 == 0 for width in PIECES)
EPS = 1e-8
TINY = 1e-30
QW, QX, QY, QZ = 0, 1, 2, 3
WINDOWS = (
    ((0, 0), (1, 0), (2, 0), (0, 1)),
    ((0, 2), (1, 1), (2, 1), (1, 2)),
    ((0, 3), (1, 3), (2, 3), (2, 2)),
)
GROUPS_OF = ((0, 1), (2, 1), (3, 2))
FIRST_WINDOW = {0: 0, 1: 0, 2: 1, 3: 2}
LAST_WINDOW = {0: 0, 1: 1, 2: 2, 3: 2}
BANK_OPENS = {0: 0, 1: 1}
BANK_CLOSES = {0: 1, 1: 2}


def tile_corrlosschamfer_kernel(tc, verts, cams, offs, out):
    nc = tc.nc
    with (
        tc.tile_pool(name="held", bufs=1) as held,
        tc.tile_pool(name="work", bufs=3 * len(PIECES)) as work,
        tc.tile_pool(name="images", bufs=len(PIECES)) as images,
        tc.psum_pool(name="sums", bufs=8) as sums,
    ):
        verts_of = verts.rearrange("(k q i h) c -> k h q i c", k=3, q=2, h=2)
        cam_rows = held.tile([SAMPLES, 7], F32, name="cam_rows")
        nc.sync.dma_start(cam_rows[:], cams)
        windows = [held.tile([128, VERTICES], F32, name=f"window{t}") for t in range(3)]
        offsets = held.tile([128, PICKS // 16], U16, name="offsets")
        for t in range(3):
            for j in range(BLOCKS):
                k, s = WINDOWS[t][j]
                nc.sync.dma_start(windows[t][j::BLOCKS, :], verts_of[k, s // 2, s % 2])
            if t == 0:
                nc.sync.dma_start(offsets[:], offs)
        quat = cam_rows[:, 3:7]
        scale = cam_rows[:, 0:1]
        quat = cam_rows[:, 3:7]

        identity = held.tile([128, 128], F32, name="identity")
        make_identity(nc, identity[:])
        by_block = identity[:].rearrange("p (i j) -> p i j", j=BLOCKS)
        by_sample = identity[:].rearrange("b (q i h) -> b h q i", q=2, h=2)
        placed = [held.tile([SAMPLES, GROUP, BLOCKS], F32, name=f"placed{t}") for t in range(3)]

        def place(t):
            for s in GROUPS_OF[t]:
                js = [j for j in range(BLOCKS) if WINDOWS[t][j][1] == s]
                into = placed[t][:, :, js[0] : js[-1] + 1 : max(1, js[-1] - js[0] - len(js) + 2)]
                nc.gpsimd.tensor_copy(into, by_sample[:, s // 2, s % 2].unsqueeze(2).to_broadcast(into.shape))

        three_one = held.tile([128, 2, GROUP], F32, name="three_one")
        two_two = held.tile([128, 2, GROUP], F32, name="two_two")
        pattern = (three_one, two_two, three_one)
        place(0)
        nc.gpsimd.tensor_tensor(two_two[:, 1, :], by_block[:, :, 1], by_block[:, :, 2], ALU.add)
        nc.gpsimd.tensor_tensor(three_one[:, 0, :], two_two[:, 1, :], by_block[:, :, 0], ALU.add)
        nc.gpsimd.tensor_copy(three_one[:, 1, :], by_block[:, :, 3])
        place(1)
        place(2)
        nc.gpsimd.tensor_tensor(two_two[:, 0, :], by_block[:, :, 0], by_block[:, :, 3], ALU.add)
        tiny = held.tile([SAMPLES, 1], F32, name="tiny")
        nc.vector.memset(tiny[:], TINY)
        early_root = held.tile([SAMPLES, 1], F32, name="early_root")
        nc.scalar.activation(early_root[:], tiny[:], ACT.Sqrt)
        ones = held.tile([128, WIDEST], F32, name="ones")
        nc.vector.memset(ones[:], 1.0)
        diagonal = held.tile([SAMPLES, 6], F32, name="diagonal")
        nc.vector.memset(diagonal[:], 0.0)
        nc.vector.memset(diagonal[:, 0:5:4], 1.0)
        masked = held.tile([128, 3, 7], F32, name="masked")
        nc.vector.memset(masked[:], TINY)
        block = held.tile([128, BLOCKS], F32, name="block")
        nc.vector.tensor_reduce(block[:], identity[:].rearrange("p (i j) -> p j i", j=BLOCKS), axis=X, op=ALU.add)
        coordinate = held.tile([128, 9], F32, name="coordinate")
        by_coordinate = coordinate[:].rearrange("p (t k) -> p t k", k=3)
        nc.vector.tensor_copy(by_coordinate, block[:, 0:3].unsqueeze(1).to_broadcast([128, 3, 3]))
        nc.vector.tensor_scalar(coordinate[:, 0:9:4], coordinate[:, 0:9:4], block[:, 3:4], None, ALU.add)

        sumsq = held.tile([SAMPLES, 1], F32, name="sumsq")
        square = held.tile([SAMPLES, 4], F32, name="square")
        nc.scalar.activation(square[:], quat, ACT.Square, accum_out=sumsq[:])
        norm = held.tile([SAMPLES, 1], F32, name="norm")
        nc.scalar.activation(norm[:], sumsq[:], ACT.Sqrt, bias=tiny[:])
        pair = held.tile([SAMPLES, 16], F32, name="pair")
        nc.vector.tensor_tensor(
            pair[:].rearrange("p (i j) -> p i j", i=4),
            quat.unsqueeze(2).to_broadcast([SAMPLES, 4, 4]),
            quat.unsqueeze(1).to_broadcast([SAMPLES, 4, 4]),
            ALU.mult,
        )

        def pr(i, j):
            return 4 * i + j

        mixed = held.tile([SAMPLES, 6], F32, name="mixed")
        nc.vector.tensor_tensor(
            mixed[:, 2:4],
            pair[:, pr(QX, QY) : pr(QX, QZ) + 1][:, ::-1],
            pair[:, pr(QY, QW) : pr(QZ, QW) + 1 : 4],
            ALU.add,
        )
        nc.vector.tensor_tensor(
            mixed[:, 1:6:4],
            pair[:, pr(QX, QY) : pr(QY, QZ) + 1 : 5],
            pair[:, pr(QW, QX) : pr(QW, QZ) + 1 : 2][:, ::-1],
            ALU.subtract,
        )
        nc.vector.tensor_scalar(
            mixed[:, 0:5:4],
            pair[:, pr(QX, QX) : pr(QY, QY) + 1 : 5][:, ::-1],
            pair[:, pr(QZ, QZ) : pr(QZ, QZ) + 1],
            -1.0,
            ALU.add,
            ALU.mult,
        )
        base = held.tile([SAMPLES, 1], F32, name="base")
        nc.vector.tensor_scalar(base[:], sumsq[:], 0.5, 0.5 * EPS * EPS, ALU.mult, ALU.add)
        halved = held.tile([SAMPLES, 1], F32, name="halved")
        nc.vector.scalar_tensor_tensor(halved[:], norm[:], EPS, base[:], ALU.mult, ALU.add)
        numer = held.tile([SAMPLES, 6], F32, name="numer")
        nc.vector.scalar_tensor_tensor(numer[:], diagonal[:], halved[:, 0:1], mixed[:], ALU.mult, ALU.add)

        moved = sums.tile([128, 3, 6], F32, name="moved", tag="bank")
        for t in range(3):
            nc.tensor.matmul(
                moved[:, t, :], placed[t][:].rearrange("b i j -> b (i j)"), numer[:], start=True, stop=True
            )
        by_rk = masked[:, :, 0:6].rearrange("p t (r k) -> p t r k", k=3)
        nc.vector.tensor_tensor(
            by_rk,
            moved[:].rearrange("p t (r k) -> p t r k", k=3),
            by_coordinate.unsqueeze(2).to_broadcast([128, 3, 2, 3]),
            ALU.mult,
        )
        pivot = held.tile([128, 3], F32, name="pivot")
        nc.vector.tensor_reduce(pivot[:], masked[:], axis=X, op=ALU.max, apply_absolute_value=True)

        own = held.tile([128, 3, 2], F32, name="own")
        nc.vector.tensor_reduce(own[:], by_rk, axis=X, op=ALU.add)
        inv_pivot = held.tile([128, 3], F32, name="inv_pivot")
        nc.vector.reciprocal(inv_pivot[:], pivot[:])
        factor = held.tile([128, 3, 2], F32, name="factor")
        nc.vector.tensor_tensor(factor[:], own[:], inv_pivot[:].unsqueeze(2).to_broadcast([128, 3, 2]), ALU.mult)
        weights = [held.tile([128, 2, 2, GROUP], F32, name=f"weights{t}") for t in range(3)]
        nc.vector.scalar_tensor_tensor(
            weights[0][:].rearrange("p r g i -> p r (g i)"),
            pattern[0][:].rearrange("p g i -> p (g i)").unsqueeze(1).to_broadcast([128, 2, 2 * GROUP]),
            inv_pivot[:, 0:1],
            own[:, 0, :].unsqueeze(2).to_broadcast([128, 2, 2 * GROUP]),
            ALU.mult,
            ALU.mult,
        )
        spread = [held.tile([128, WIDEST], F32, name=f"spread{t}") for t in range(3)]
        nc.vector.tensor_scalar(spread[0][:], ones[:], pivot[:, 0:1], None, ALU.mult)
        for t in (1, 2):
            nc.scalar.activation(spread[t][:], pivot[:, t : t + 1].to_broadcast([128, WIDEST]), ACT.Identity)
            for r in range(2):
                nc.scalar.activation(weights[t][:, r, :, :], pattern[t][:], ACT.Identity, scale=factor[:, t, r : r + 1])

        finish = held.tile([SAMPLES, 4], F32, name="finish")
        nc.scalar.activation(finish[:, 0:4:2], cam_rows[:, 1:3], ACT.Identity)
        inv_halved = held.tile([SAMPLES, 1], F32, name="inv_halved")
        nc.vector.reciprocal(inv_halved[:], halved[:])
        nc.vector.tensor_scalar(finish[:, 1:4:2], inv_halved[:].to_broadcast([SAMPLES, 2]), scale, None, ALU.mult)
        moved_finish = sums.tile([128, 2, 2], F32, name="moved_finish", tag="bank")
        for h in range(2):
            for r in range(2):
                for q in range(2):
                    quadrant = 2 * r + q
                    nc.tensor.matmul(
                        moved_finish[quadrant * GROUP : (quadrant + 1) * GROUP, h, :],
                        by_sample[:, h, q],
                        finish[:, 2 * r : 2 * r + 2],
                        start=True,
                        stop=True,
                    )
        bank_finish = held.tile([128, 2, 2], F32, name="bank_finish")
        nc.scalar.activation(bank_finish[:], moved_finish[:], ACT.Identity)

        out_of = out.rearrange("(m h) c -> m h c", h=2)
        starts = [sum(PIECES[:n]) for n in range(len(PIECES))]
        total = {}
        for t in range(3):
            for n, width in enumerate(PIECES):
                columns = slice(starts[n], starts[n] + width)
                picked = work.tile([128, width], F32, name="picked")
                nc.vector.tensor_tensor(
                    picked[:],
                    windows[t][:].indirect(offsets[:, starts[n] // 16 : (starts[n] + width) // 16]),
                    spread[t][:, 0:width],
                    ALU.mult,
                )
                for h in range(2):
                    if BANK_OPENS[h] == t:
                        total[n, h] = sums.tile([128, width], F32, name=f"total{h}", tag="bank")
                for g, s in enumerate(GROUPS_OF[t]):
                    h, q = s // 2, s % 2
                    for r in range(2):
                        quadrant = 2 * r + q
                        nc.tensor.matmul(
                            total[n, h][quadrant * GROUP : (quadrant + 1) * GROUP, :],
                            weights[t][:, r, g, :],
                            picked[:],
                            start=(t == FIRST_WINDOW[s]),
                            stop=(t == LAST_WINDOW[s]),
                        )
                for h in range(2):
                    if BANK_CLOSES[h] == t:
                        image = images.tile([128, width], F32, name=f"image{h}")
                        nc.scalar.activation(image[:], total[n, h][:], ACT.Identity, bias=bank_finish[:, h, 0:1], scale=bank_finish[:, h, 1:2])
                        nc.sync.dma_start(out_of[:, h, columns], image[:])
